import numpy as np
import ml_dtypes


def mxq(x, axis, fmt="e4m3"):
    dtype, down = {"e4m3": (ml_dtypes.float8_e4m3fn, 7), "e5m2": (ml_dtypes.float8_e5m2, 14)}[fmt]
    v = np.moveaxis(np.asarray(x, np.float32).astype(ml_dtypes.bfloat16).astype(np.float64), axis, -1)
    blocks = v.reshape(v.shape[:-1] + (-1, 32))
    amax = np.abs(blocks).max(-1, keepdims=True)
    byte = np.maximum(np.where(amax > 0, np.frexp(amax)[1] - 1 + 127, 0) - down, 1)
    scale = np.exp2(byte - 127.0)
    codes = (blocks / scale).astype(np.float32).astype(dtype).astype(np.float64)
    return np.moveaxis((codes * scale).reshape(v.shape), -1, axis)


WIDE = False


def mx_kscale(k):
    if not WIDE:
        return np.ones(k)
    levels = np.array([10, -10, 5, -5, 0])
    a = np.random.permutation(np.resize(levels, k // 512 * 4)).reshape(k // 512, 4)
    idx = np.arange(k)
    return np.exp2(a[idx // 512, idx % 128 // 32])


BF16 = ml_dtypes.bfloat16


def bf(x):
    return np.asarray(x, np.float32).astype(BF16)


def f64(x):
    return np.asarray(x).astype(np.float64)


E2M1 = np.array([0.0, 0.5, 1.0, 1.5, 2.0, 3.0, 4.0, 6.0, -0.0, -0.5, -1.0, -1.5, -2.0, -3.0, -4.0, -6.0])


def pack_weight(w, fmt):
    k, n = w.shape
    w = f64(bf(w)).reshape(k // 32, 32, n)
    amax = np.abs(w).max(1)
    if fmt == "e4m3":
        byte = np.frexp(amax)[1] - 1 + 127 - 7
    else:
        mant, ex = np.frexp(amax / 6.0)
        byte = np.where(mant > 0.5, ex, ex - 1) + 127
    byte = np.clip(np.where(amax > 0, byte, 1), 1, 254)
    scaled = (w * np.exp2(127.0 - byte)[:, None, :]).reshape(k, n).astype(np.float32)
    by_word = np.ascontiguousarray(scaled.reshape(k // 512, 128, 4, n).transpose(0, 1, 3, 2))
    if fmt == "e4m3":
        words = by_word.astype(ml_dtypes.float8_e4m3fn).view(np.uint8)
    else:
        c = by_word.astype(ml_dtypes.float4_e2m1fn).view(np.uint8) & 0xF
        words = c[..., 0::2] | (c[..., 1::2] << 4)
    return np.ascontiguousarray(words), np.ascontiguousarray(byte.astype(np.uint8).reshape(k // 512, 16, n))


def unpack_weight(words, scales, fmt):
    g, p, n, _ = words.shape
    if fmt == "e4m3":
        vals = np.ascontiguousarray(words).view(ml_dtypes.float8_e4m3fn).astype(np.float64)
    else:
        nib = np.empty((g, p, n, 4), np.uint8)
        nib[..., 0::2] = words & 0xF
        nib[..., 1::2] = words >> 4
        vals = E2M1[nib]
    vals = vals * np.repeat(np.exp2(scales.astype(np.float64) - 127.0), 8, axis=1)[..., None]
    return vals.transpose(0, 1, 3, 2).reshape(g * 512, n)


B, S, HID, H, KV, D = 1, 512, 2048, 16, 4, 128
EPS = 1e-6
THETA = 10000.0
HALF = D // 2
FMT = "e4m3"


def rotate_half(x):
    return np.concatenate([-x[..., HALF:], x[..., :HALF]], axis=-1)


def rms_norm(x, w=None):
    n = x * (1.0 / np.sqrt(np.mean(x * x, axis=-1, keepdims=True) + EPS))
    return n if w is None else n * w


def setup_inputs():
    s = mx_kscale(HID)
    c = 0.004 / np.sqrt(HID)
    inv_freq = 1.0 / THETA ** (np.arange(0, D, 2) / D)
    pos = np.random.randint(0, S) + np.arange(S)
    freqs = pos[:, None] * inv_freq[None, :]
    emb = np.concatenate([freqs, freqs], axis=-1)
    hidden_states = bf(np.random.standard_normal((B, S, HID)) * s)
    Wq_words, Wq_scales = pack_weight((np.random.standard_normal((H * D, HID)) * c / s[None, :]).T, FMT)
    Wk_words, Wk_scales = pack_weight((np.random.standard_normal((KV * D, HID)) * c / s[None, :]).T, FMT)
    Wv_words, Wv_scales = pack_weight((np.random.standard_normal((KV * D, HID)) * c / s[None, :]).T, FMT)
    return {"hidden_states": hidden_states,
            "cos": bf(np.cos(emb)[None]),
            "sin": bf(np.sin(emb)[None]),
            "Wq_words": Wq_words,
            "Wq_scales": Wq_scales,
            "Wk_words": Wk_words,
            "Wk_scales": Wk_scales,
            "Wv_words": Wv_words,
            "Wv_scales": Wv_scales,
            "q_norm_w": bf(0.5 + 0.1 * np.random.standard_normal(D)),
            "k_norm_w": bf(0.5 + 0.1 * np.random.standard_normal(D))}


def reference(hidden_states, cos, sin, Wq_words, Wq_scales, Wk_words, Wk_scales, Wv_words, Wv_scales, q_norm_w, k_norm_w):
    xq = mxq(f64(hidden_states), 2, "e4m3")
    cs = f64(cos)[:, :, None, :]
    sn = f64(sin)[:, :, None, :]
    q = (xq @ unpack_weight(Wq_words, Wq_scales, FMT)).reshape(B, S, H, D)
    k = (xq @ unpack_weight(Wk_words, Wk_scales, FMT)).reshape(B, S, KV, D)
    v = (xq @ unpack_weight(Wv_words, Wv_scales, FMT)).reshape(B, S, KV, D)
    q = rms_norm(q, f64(q_norm_w))
    q = q * cs + rotate_half(q) * sn
    k = rms_norm(k, f64(k_norm_w))
    k = k * cs + rotate_half(k) * sn
    v = rms_norm(v)
    return q.transpose(0, 2, 1, 3), k.transpose(0, 2, 1, 3), v.transpose(0, 2, 1, 3)

@@ -1,0 +1,231 @@
+from contextlib import ExitStack
+
+import concourse.mybir as mybir
+from concourse.masks import make_identity
+
+F32 = mybir.dt.float32
+BF16 = mybir.dt.bfloat16
+I32 = mybir.dt.int32
+U32 = mybir.dt.uint32
+U8 = mybir.dt.uint8
+FP8X4 = mybir.dt.float8_e4m3fn_x4
+ACT = mybir.ActivationFunctionType
+ALU = mybir.AluOpType
+
+P = 128
+TOKENS = 512
+HID = 2048
+D = 128
+HALF = D // 2
+EPS = 1e-6
+K_PASS = 4 * P
+PASSES = HID // K_PASS
+TOKEN_TILES = TOKENS // P
+BANK = 512
+HEADS_PER_BANK = BANK // D
+Q_FEATURES = 2048
+KV_FEATURES = 512
+FEATURES = Q_FEATURES + 2 * KV_FEATURES
+GROUPS = FEATURES // BANK
+Q_GROUPS = Q_FEATURES // BANK
+WORDS_PER_PASS = K_PASS // 2
+
+FLOPS = 2 * TOKENS * HID * FEATURES
+
+
+def tile_refattention_pa_kernel(
+    tc,
+    hidden_states,
+    cos,
+    sin,
+    Wq_words,
+    Wq_scales,
+    Wk_words,
+    Wk_scales,
+    Wv_words,
+    Wv_scales,
+    q_norm_w,
+    k_norm_w,
+    out_0,
+    out_1,
+    out_2,
+):
+    nc = tc.nc
+    with ExitStack() as ctx:
+        ctx.enter_context(tc.manual_schedule())
+        keep = ctx.enter_context(tc.tile_pool(name="keep", bufs=1))
+        stage = ctx.enter_context(tc.tile_pool(name="stage", bufs=4))
+        small = ctx.enter_context(tc.tile_pool(name="small", bufs=6))
+        junk = ctx.enter_context(tc.tile_pool(name="junk", bufs=4))
+        work = ctx.enter_context(tc.tile_pool(name="work", bufs=3))
+        outs = ctx.enter_context(tc.tile_pool(name="outs", bufs=4))
+        psum = ctx.enter_context(tc.psum_pool(name="psum", bufs=8))
+
+        x_dram = hidden_states.rearrange("b (p j) k -> p (b j) k", j=TOKEN_TILES)
+        cos_dram = cos.rearrange("b (p j) d -> p (b j) d", j=TOKEN_TILES)
+        sin_dram = sin.rearrange("b (p j) d -> p (b j) d", j=TOKEN_TILES)
+
+        x_sb = keep.tile([P, TOKEN_TILES, HID], BF16, name="x_sb")
+        cos_sb = keep.tile([P, TOKEN_TILES, D], BF16, name="cos_sb")
+        sin_sb = keep.tile([P, TOKEN_TILES, D], BF16, name="sin_sb")
+        gain = keep.tile([P, 2, D], BF16, name="gain")
+        w_words = keep.tile([P, GROUPS, PASSES, BANK], U32, name="w_words", align_bytes=64)
+        w_planes = keep.tile([P, FEATURES], U8, name="w_planes", align_bytes=64)
+        x_codes = keep.tile([P, TOKEN_TILES, PASSES, P], U32, name="x_codes", align_bytes=64)
+        x_planes = keep.tile([P, TOKEN_TILES, PASSES, P], U8, name="x_planes", align_bytes=64)
+        rope = keep.tile([P, TOKEN_TILES, 2, 2, D], F32, name="rope")
+        ident = keep.tile([P, P], F32, name="ident")
+        one = keep.tile([P, 1], F32, name="one")
+        warm = keep.tile([P, 1], F32, name="warm")
+
+        nc.vector.memset(w_planes[:].bitcast(I32), 0)
+        nc.vector.memset(one[:], 1.0)
+        make_identity(nc, ident[:])
+
+        nc.scalar.dma_start(out=cos_sb[:], in_=cos_dram)
+        nc.scalar.dma_start(out=sin_sb[:], in_=sin_dram)
+        nc.scalar.dma_start(out=gain[:, 0, :], in_=q_norm_w.partition_broadcast(P))
+        nc.scalar.dma_start(out=gain[:, 1, :], in_=k_norm_w.partition_broadcast(P))
+        nc.scalar.activation(out=warm[:], in_=one[:], func=ACT.Abs_reciprocal_sqrt)
+
+        for j in range(TOKEN_TILES):
+            nc.sync.dma_start(out=x_sb[:, j, :], in_=x_dram[:, j, :])
+
+        def load_scales(scales, first_feature, features):
+            for quadrant in range(4):
+                nc.sync.dma_start(
+                    out=w_planes[
+                        32 * quadrant : 32 * quadrant + 16, first_feature : first_feature + features
+                    ].bitcast(I32),
+                    in_=scales[:, 4 * quadrant : 4 * quadrant + 4, :].bitcast(I32),
+                )
+
+        def load_words(words, group, first_column):
+            by_partition = words.rearrange("g p n t -> p g (n t)")
+            for g in range(PASSES):
+                nc.sync.dma_start(
+                    out=w_words[:, group, g, :].bitcast(I32),
+                    in_=by_partition[:, g, 4 * first_column : 4 * (first_column + BANK)].bitcast(I32),
+                )
+
+        load_scales(Wq_scales, 0, Q_FEATURES)
+        for group in range(Q_GROUPS):
+            load_words(Wq_words, group, group * BANK)
+        load_scales(Wk_scales, Q_FEATURES, KV_FEATURES)
+        load_scales(Wv_scales, Q_FEATURES + KV_FEATURES, KV_FEATURES)
+        load_words(Wk_words, Q_GROUPS, 0)
+        load_words(Wv_words, Q_GROUPS + 1, 0)
+
+        for j in range(TOKEN_TILES):
+            x_words = x_sb[:, j, :].bitcast(F32)
+            for pair in range(PASSES // 2):
+                turned = psum.tile([P, 2, 2, P], F32, tag="bank", name="turned")
+                for gi in range(2):
+                    g = 2 * pair + gi
+                    for u in range(2):
+                        nc.tensor.transpose(
+                            turned[:, gi, u, :],
+                            x_words[:, WORDS_PER_PASS * g + u : WORDS_PER_PASS * (g + 1) : 2],
+                            ident[:],
+                        )
+                grouped = stage.tile([P, 2, P, 4], BF16, name="grouped", align_bytes=64)
+                nc.scalar.copy(
+                    out=grouped[:].bitcast(F32),
+                    in_=turned[:].rearrange("p g u r -> p g r u"),
+                )
+                nc.vector.quantize_mx(
+                    out=x_codes[:, j, 2 * pair : 2 * pair + 2, :]
+                    .rearrange("p g r -> p (g r)")
+                    .bitcast(FP8X4),
+                    scales=x_planes[:, j, 2 * pair : 2 * pair + 2, :].rearrange("p g r -> p (g r)"),
+                    in_=grouped[:].rearrange("p g r t -> p (g r t)"),
+                )
+            nc.vector.tensor_tensor(
+                out=rope[:, j, :, 0, :],
+                in0=cos_sb[:, j, :].unsqueeze(1).to_broadcast([P, 2, D]),
+                in1=gain[:],
+                op=ALU.mult,
+            )
+            nc.vector.tensor_tensor(
+                out=rope[:, j, :, 1, 0:HALF],
+                in0=sin_sb[:, j, HALF:D].unsqueeze(1).to_broadcast([P, 2, HALF]),
+                in1=gain[:, :, 0:HALF],
+                op=ALU.mult,
+            )
+            nc.vector.scalar_tensor_tensor(
+                out=rope[:, j, :, 1, HALF:D],
+                in0=sin_sb[:, j, 0:HALF].unsqueeze(1).to_broadcast([P, 2, HALF]),
+                scalar=-1.0,
+                in1=gain[:, :, HALF:D],
+                op0=ALU.mult,
+                op1=ALU.mult,
+            )
+
+        out_views = [
+            out_0[:, HEADS_PER_BANK * group : HEADS_PER_BANK * (group + 1)] for group in range(Q_GROUPS)
+        ] + [out_1, out_2]
+        for group in range(GROUPS):
+            out_view = out_views[group].rearrange("b h (p j) d -> p (b h) j d", j=TOKEN_TILES)
+            rotary = group < GROUPS - 1
+            for pair in range(TOKEN_TILES // 2):
+                result = outs.tile([P, HEADS_PER_BANK, 2, D], F32, name="result")
+                if rotary:
+                    products = work.tile([P, HEADS_PER_BANK, 2, 2, D], F32, name="products")
+                for jj in range(2):
+                    j = 2 * pair + jj
+                    acc = psum.tile([P, HEADS_PER_BANK, D], F32, tag="bank", name="acc")
+                    for g in range(PASSES):
+                        nc.tensor.matmul_mx(
+                            out=acc[:].rearrange("p h d -> p (h d)"),
+                            lhsT=x_codes[:, j, g, :].bitcast(FP8X4),
+                            lhsT_scale=x_planes[:, j, g, :],
+                            rhs=w_words[:, group, g, :].bitcast(FP8X4),
+                            rhs_scale=w_planes[4 * g : P, BANK * group : BANK * (group + 1)],
+                            start=(g == 0),
+                            stop=(g == PASSES - 1),
+                        )
+                    squares = junk.tile([P, HEADS_PER_BANK, D], F32, name="squares")
+                    sum_sq = small.tile([P, HEADS_PER_BANK], F32, name="sum_sq")
+                    for h in range(HEADS_PER_BANK):
+                        nc.scalar.activation(
+                            out=squares[:, h, :],
+                            in_=acc[:, h, :],
+                            func=ACT.Square,
+                            accum_out=sum_sq[:, h : h + 1],
+                        )
+                    rstd = small.tile([P, HEADS_PER_BANK], F32, name="rstd")
+                    nc.scalar.activation(
+                        out=rstd[:], in_=sum_sq[:], func=ACT.Abs_reciprocal_sqrt, scale=1.0 / D, bias=EPS
+                    )
+                    if rotary:
+                        which = 0 if group < Q_GROUPS else 1
+                        for h in range(HEADS_PER_BANK):
+                            nc.vector.scalar_tensor_tensor(
+                                out=products[:, h, jj, :, :],
+                                in0=acc[:, h, :].unsqueeze(1).to_broadcast([P, 2, D]),
+                                scalar=rstd[:, h : h + 1],
+                                in1=rope[:, j, which, :, :],
+                                op0=ALU.mult,
+                                op1=ALU.mult,
+                            )
+                    else:
+                        nc.vector.tensor_tensor(
+                            out=result[:, :, jj, :],
+                            in0=acc[:],
+                            in1=rstd[:].unsqueeze(2).to_broadcast([P, HEADS_PER_BANK, D]),
+                            op=ALU.mult,
+                        )
+                if rotary:
+                    nc.gpsimd.tensor_tensor(
+                        out=result[:, :, :, 0:HALF],
+                        in0=products[:, :, :, 0, 0:HALF],
+                        in1=products[:, :, :, 1, HALF:D],
+                        op=ALU.add,
+                    )
+                    nc.gpsimd.tensor_tensor(
+                        out=result[:, :, :, HALF:D],
+                        in0=products[:, :, :, 0, HALF:D],
+                        in1=products[:, :, :, 1, 0:HALF],
+                        op=ALU.add,
+                    )
+                nc.sync.dma_start(out=out_view[:, :, 2 * pair : 2 * pair + 2, :], in_=result[:])

@@ -68,7 +68,8 @@ def tile_refattention_pa_kernel(
         x_sb = keep.tile([P, TOKEN_TILES, HID], BF16, name="x_sb")
         cos_sb = keep.tile([P, TOKEN_TILES, D], BF16, name="cos_sb")
         sin_sb = keep.tile([P, TOKEN_TILES, D], BF16, name="sin_sb")
-        gain = keep.tile([P, 2, D], BF16, name="gain")
+        gain_rows = keep.tile([P, 2, D], BF16, name="gain_rows")
+        ones = keep.tile([P, P], BF16, name="ones")
         w_words = keep.tile([P, GROUPS, PASSES, BANK], U32, name="w_words", align_bytes=64)
         w_planes = keep.tile([P, FEATURES], U8, name="w_planes", align_bytes=64)
         x_codes = keep.tile([P, TOKEN_TILES, PASSES, P], U32, name="x_codes", align_bytes=64)
@@ -80,12 +81,14 @@ def tile_refattention_pa_kernel(
 
         nc.vector.memset(w_planes[:].bitcast(I32), 0)
         nc.vector.memset(one[:], 1.0)
+        nc.vector.memset(gain_rows[:], 0.0)
+        nc.vector.memset(ones[:], 1.0)
         make_identity(nc, ident[:])
 
+        nc.scalar.dma_start(out=gain_rows[0:1, 0, :], in_=q_norm_w.rearrange("(o d) -> o d", o=1))
+        nc.scalar.dma_start(out=gain_rows[0:1, 1, :], in_=k_norm_w.rearrange("(o d) -> o d", o=1))
         nc.scalar.dma_start(out=cos_sb[:], in_=cos_dram)
         nc.scalar.dma_start(out=sin_sb[:], in_=sin_dram)
-        nc.scalar.dma_start(out=gain[:, 0, :], in_=q_norm_w.partition_broadcast(P))
-        nc.scalar.dma_start(out=gain[:, 1, :], in_=k_norm_w.partition_broadcast(P))
         nc.scalar.activation(out=warm[:], in_=one[:], func=ACT.Abs_reciprocal_sqrt)
 
         for j in range(TOKEN_TILES):
@@ -115,6 +118,15 @@ def tile_refattention_pa_kernel(
         load_scales(Wv_scales, Q_FEATURES + KV_FEATURES, KV_FEATURES)
         load_words(Wk_words, Q_GROUPS, 0)
         load_words(Wv_words, Q_GROUPS + 1, 0)
+
+        gain = psum.tile([P, 2, D], F32, tag="bank", name="gain")
+        nc.tensor.matmul(
+            out=gain[:].rearrange("p w d -> p (w d)"),
+            lhsT=ones[:],
+            rhs=gain_rows[:].rearrange("p w d -> p (w d)"),
+            start=True,
+            stop=True,
+        )
 
         for j in range(TOKEN_TILES):
             x_words = x_sb[:, j, :].bitcast(F32)

@@ -57,8 +57,8 @@ def tile_refattention_pa_kernel(
         stage = ctx.enter_context(tc.tile_pool(name="stage", bufs=4))
         small = ctx.enter_context(tc.tile_pool(name="small", bufs=6))
         junk = ctx.enter_context(tc.tile_pool(name="junk", bufs=4))
-        work = ctx.enter_context(tc.tile_pool(name="work", bufs=3))
-        outs = ctx.enter_context(tc.tile_pool(name="outs", bufs=4))
+        work = ctx.enter_context(tc.tile_pool(name="work", bufs=5))
+        outs = ctx.enter_context(tc.tile_pool(name="outs", bufs=8))
         psum = ctx.enter_context(tc.psum_pool(name="psum", bufs=8))
 
         x_dram = hidden_states.rearrange("b (p j) k -> p (b j) k", j=TOKEN_TILES)
@@ -119,15 +119,6 @@ def tile_refattention_pa_kernel(
         load_words(Wk_words, Q_GROUPS, 0)
         load_words(Wv_words, Q_GROUPS + 1, 0)
 
-        gain = psum.tile([P, 2, D], F32, tag="bank", name="gain")
-        nc.tensor.matmul(
-            out=gain[:].rearrange("p w d -> p (w d)"),
-            lhsT=ones[:],
-            rhs=gain_rows[:].rearrange("p w d -> p (w d)"),
-            start=True,
-            stop=True,
-        )
-
         for j in range(TOKEN_TILES):
             x_words = x_sb[:, j, :].bitcast(F32)
             for pair in range(PASSES // 2):
@@ -152,6 +143,16 @@ def tile_refattention_pa_kernel(
                     scales=x_planes[:, j, 2 * pair : 2 * pair + 2, :].rearrange("p g r -> p (g r)"),
                     in_=grouped[:].rearrange("p g r t -> p (g r t)"),
                 )
+
+        gain = psum.tile([P, 2, D], F32, tag="bank", name="gain")
+        nc.tensor.matmul(
+            out=gain[:].rearrange("p w d -> p (w d)"),
+            lhsT=ones[:],
+            rhs=gain_rows[:].rearrange("p w d -> p (w d)"),
+            start=True,
+            stop=True,
+        )
+        for j in range(TOKEN_TILES):
             nc.vector.tensor_tensor(
                 out=rope[:, j, :, 0, :],
                 in0=cos_sb[:, j, :].unsqueeze(1).to_broadcast([P, 2, D]),
@@ -228,13 +229,14 @@ def tile_refattention_pa_kernel(
                             op=ALU.mult,
                         )
                 if rotary:
-                    nc.gpsimd.tensor_tensor(
+                    adder = nc.gpsimd if group < Q_GROUPS else nc.vector
+                    adder.tensor_tensor(
                         out=result[:, :, :, 0:HALF],
                         in0=products[:, :, :, 0, 0:HALF],
                         in1=products[:, :, :, 1, HALF:D],
                         op=ALU.add,
                     )
-                    nc.gpsimd.tensor_tensor(
+                    adder.tensor_tensor(
                         out=result[:, :, :, HALF:D],
                         in0=products[:, :, :, 0, HALF:D],
                         in1=products[:, :, :, 1, 0:HALF],

@@ -229,17 +229,11 @@ def tile_refattention_pa_kernel(
                             op=ALU.mult,
                         )
                 if rotary:
-                    adder = nc.gpsimd if group < Q_GROUPS else nc.vector
-                    adder.tensor_tensor(
-                        out=result[:, :, :, 0:HALF],
-                        in0=products[:, :, :, 0, 0:HALF],
-                        in1=products[:, :, :, 1, HALF:D],
-                        op=ALU.add,
-                    )
-                    adder.tensor_tensor(
-                        out=result[:, :, :, HALF:D],
-                        in0=products[:, :, :, 0, HALF:D],
-                        in1=products[:, :, :, 1, 0:HALF],
+                    halves = products[:].rearrange("p h j s (f i) -> p (h j) s f i", f=2)
+                    nc.gpsimd.tensor_tensor(
+                        out=result[:].rearrange("p h j (f i) -> p (h j) f i", f=2),
+                        in0=halves[:, :, 0, :, :],
+                        in1=halves[:, :, 1, ::-1, :],
                         op=ALU.add,
                     )
                 nc.sync.dma_start(out=out_view[:, :, 2 * pair : 2 * pair + 2, :], in_=result[:])

@@ -221,13 +221,21 @@ def tile_refattention_pa_kernel(
                                 op0=ALU.mult,
                                 op1=ALU.mult,
                             )
-                    else:
+                    elif jj == 0:
                         nc.vector.tensor_tensor(
                             out=result[:, :, jj, :],
                             in0=acc[:],
                             in1=rstd[:].unsqueeze(2).to_broadcast([P, HEADS_PER_BANK, D]),
                             op=ALU.mult,
                         )
+                    else:
+                        for h in range(HEADS_PER_BANK):
+                            nc.scalar.activation(
+                                out=result[:, h, jj, :],
+                                in_=acc[:, h, :],
+                                func=ACT.Copy,
+                                scale=rstd[:, h : h + 1],
+                            )
                 if rotary:
                     halves = products[:].rearrange("p h j s (f i) -> p (h j) s f i", f=2)
                     nc.gpsimd.tensor_tensor(
@@ -236,4 +244,9 @@ def tile_refattention_pa_kernel(
                         in1=halves[:, :, 1, ::-1, :],
                         op=ALU.add,
                     )
-                nc.sync.dma_start(out=out_view[:, :, 2 * pair : 2 * pair + 2, :], in_=result[:])
+                if group == GROUPS - 2 and pair == TOKEN_TILES // 2 - 1:
+                    last_rotary_view = out_view[:, :, 2 * pair : 2 * pair + 2, :]
+                    last_rotary_result = result
+                else:
+                    nc.sync.dma_start(out=out_view[:, :, 2 * pair : 2 * pair + 2, :], in_=result[:])
+        nc.sync.dma_start(out=last_rotary_view, in_=last_rotary_result[:])

@@ -52,7 +52,6 @@ def tile_refattention_pa_kernel(
 ):
     nc = tc.nc
     with ExitStack() as ctx:
-        ctx.enter_context(tc.manual_schedule())
         keep = ctx.enter_context(tc.tile_pool(name="keep", bufs=1))
         stage = ctx.enter_context(tc.tile_pool(name="stage", bufs=4))
         small = ctx.enter_context(tc.tile_pool(name="small", bufs=6))
@@ -221,21 +220,13 @@ def tile_refattention_pa_kernel(
                                 op0=ALU.mult,
                                 op1=ALU.mult,
                             )
-                    elif jj == 0:
+                    else:
                         nc.vector.tensor_tensor(
                             out=result[:, :, jj, :],
                             in0=acc[:],
                             in1=rstd[:].unsqueeze(2).to_broadcast([P, HEADS_PER_BANK, D]),
                             op=ALU.mult,
                         )
-                    else:
-                        for h in range(HEADS_PER_BANK):
-                            nc.scalar.activation(
-                                out=result[:, h, jj, :],
-                                in_=acc[:, h, :],
-                                func=ACT.Copy,
-                                scale=rstd[:, h : h + 1],
-                            )
                 if rotary:
                     halves = products[:].rearrange("p h j s (f i) -> p (h j) s f i", f=2)
                     nc.gpsimd.tensor_tensor(
@@ -244,9 +235,4 @@ def tile_refattention_pa_kernel(
                         in1=halves[:, :, 1, ::-1, :],
                         op=ALU.add,
                     )
-                if group == GROUPS - 2 and pair == TOKEN_TILES // 2 - 1:
-                    last_rotary_view = out_view[:, :, 2 * pair : 2 * pair + 2, :]
-                    last_rotary_result = result
-                else:
-                    nc.sync.dma_start(out=out_view[:, :, 2 * pair : 2 * pair + 2, :], in_=result[:])
-        nc.sync.dma_start(out=last_rotary_view, in_=last_rotary_result[:])
+                nc.sync.dma_start(out=out_view[:, :, 2 * pair : 2 * pair + 2, :], in_=result[:])

@@ -57,7 +57,7 @@ def tile_refattention_pa_kernel(
         small = ctx.enter_context(tc.tile_pool(name="small", bufs=6))
         junk = ctx.enter_context(tc.tile_pool(name="junk", bufs=4))
         work = ctx.enter_context(tc.tile_pool(name="work", bufs=5))
-        outs = ctx.enter_context(tc.tile_pool(name="outs", bufs=8))
+        outs = ctx.enter_context(tc.tile_pool(name="outs", bufs=4))
         psum = ctx.enter_context(tc.psum_pool(name="psum", bufs=8))
 
         x_dram = hidden_states.rearrange("b (p j) k -> p (b j) k", j=TOKEN_TILES)
@@ -69,7 +69,7 @@ def tile_refattention_pa_kernel(
         sin_sb = keep.tile([P, TOKEN_TILES, D], BF16, name="sin_sb")
         gain_rows = keep.tile([P, 2, D], BF16, name="gain_rows")
         ones = keep.tile([P, P], BF16, name="ones")
-        w_words = keep.tile([P, GROUPS, PASSES, BANK], U32, name="w_words", align_bytes=64)
+        w_words = keep.tile([P, PASSES, FEATURES], U32, name="w_words", align_bytes=64)
         w_planes = keep.tile([P, FEATURES], U8, name="w_planes", align_bytes=64)
         x_codes = keep.tile([P, TOKEN_TILES, PASSES, P], U32, name="x_codes", align_bytes=64)
         x_planes = keep.tile([P, TOKEN_TILES, PASSES, P], U8, name="x_planes", align_bytes=64)
@@ -102,21 +102,28 @@ def tile_refattention_pa_kernel(
                     in_=scales[:, 4 * quadrant : 4 * quadrant + 4, :].bitcast(I32),
                 )
 
-        def load_words(words, group, first_column):
+        def load_words(words, first_feature, first_column, columns, by_pass=False):
             by_partition = words.rearrange("g p n t -> p g (n t)")
-            for g in range(PASSES):
+            if by_pass:
+                for g in range(PASSES):
+                    nc.sync.dma_start(
+                        out=w_words[:, g, first_feature : first_feature + columns].bitcast(I32),
+                        in_=by_partition[:, g, 4 * first_column : 4 * (first_column + columns)].bitcast(I32),
+                    )
+            else:
                 nc.sync.dma_start(
-                    out=w_words[:, group, g, :].bitcast(I32),
-                    in_=by_partition[:, g, 4 * first_column : 4 * (first_column + BANK)].bitcast(I32),
+                    out=w_words[:, :, first_feature : first_feature + columns].bitcast(I32),
+                    in_=by_partition[:, :, 4 * first_column : 4 * (first_column + columns)].bitcast(I32),
                 )
 
         load_scales(Wq_scales, 0, Q_FEATURES)
-        for group in range(Q_GROUPS):
-            load_words(Wq_words, group, group * BANK)
+        load_words(Wq_words, 0, 0, BANK, by_pass=True)
+        load_words(Wq_words, BANK, BANK, BANK)
+        load_words(Wq_words, 2 * BANK, 2 * BANK, 2 * BANK)
         load_scales(Wk_scales, Q_FEATURES, KV_FEATURES)
         load_scales(Wv_scales, Q_FEATURES + KV_FEATURES, KV_FEATURES)
-        load_words(Wk_words, Q_GROUPS, 0)
-        load_words(Wv_words, Q_GROUPS + 1, 0)
+        load_words(Wk_words, Q_FEATURES, 0, KV_FEATURES)
+        load_words(Wv_words, Q_FEATURES + KV_FEATURES, 0, KV_FEATURES)
 
         for j in range(TOKEN_TILES):
             x_words = x_sb[:, j, :].bitcast(F32)
@@ -179,10 +186,11 @@ def tile_refattention_pa_kernel(
         for group in range(GROUPS):
             out_view = out_views[group].rearrange("b h (p j) d -> p (b h) j d", j=TOKEN_TILES)
             rotary = group < GROUPS - 1
+            whole_store = group < Q_GROUPS
+            result = outs.tile([P, HEADS_PER_BANK, TOKEN_TILES, D], F32, name="result")
             for pair in range(TOKEN_TILES // 2):
-                result = outs.tile([P, HEADS_PER_BANK, 2, D], F32, name="result")
                 if rotary:
-                    products = work.tile([P, HEADS_PER_BANK, 2, 2, D], F32, name="products")
+                    products = work.tile([P, HEADS_PER_BANK, 4, D], F32, name="products")
                 for jj in range(2):
                     j = 2 * pair + jj
                     acc = psum.tile([P, HEADS_PER_BANK, D], F32, tag="bank", name="acc")
@@ -191,7 +199,7 @@ def tile_refattention_pa_kernel(
                             out=acc[:].rearrange("p h d -> p (h d)"),
                             lhsT=x_codes[:, j, g, :].bitcast(FP8X4),
                             lhsT_scale=x_planes[:, j, g, :],
-                            rhs=w_words[:, group, g, :].bitcast(FP8X4),
+                            rhs=w_words[:, g, BANK * group : BANK * (group + 1)].bitcast(FP8X4),
                             rhs_scale=w_planes[4 * g : P, BANK * group : BANK * (group + 1)],
                             start=(g == 0),
                             stop=(g == PASSES - 1),
@@ -213,7 +221,7 @@ def tile_refattention_pa_kernel(
                         which = 0 if group < Q_GROUPS else 1
                         for h in range(HEADS_PER_BANK):
                             nc.vector.scalar_tensor_tensor(
-                                out=products[:, h, jj, :, :],
+                                out=products[:, h, jj : 4 - jj : 3 - 2 * jj, :],
                                 in0=acc[:, h, :].unsqueeze(1).to_broadcast([P, 2, D]),
                                 scalar=rstd[:, h : h + 1],
                                 in1=rope[:, j, which, :, :],
@@ -222,17 +230,23 @@ def tile_refattention_pa_kernel(
                             )
                     else:
                         nc.vector.tensor_tensor(
-                            out=result[:, :, jj, :],
+                            out=result[:, :, j, :],
                             in0=acc[:],
                             in1=rstd[:].unsqueeze(2).to_broadcast([P, HEADS_PER_BANK, D]),
                             op=ALU.mult,
                         )
                 if rotary:
-                    halves = products[:].rearrange("p h j s (f i) -> p (h j) s f i", f=2)
+                    halves = products[:].rearrange("p h q (f i) -> p h (q f) i", f=2)
                     nc.gpsimd.tensor_tensor(
-                        out=result[:].rearrange("p h j (f i) -> p (h j) f i", f=2),
-                        in0=halves[:, :, 0, :, :],
-                        in1=halves[:, :, 1, ::-1, :],
+                        out=result[:, :, 2 * pair : 2 * pair + 2, :].rearrange("p h j (f i) -> p h (j f) i", f=2),
+                        in0=halves[:, :, 0:4, :],
+                        in1=halves[:, :, 7:3:-1, :],
                         op=ALU.add,
                     )
-                nc.sync.dma_start(out=out_view[:, :, 2 * pair : 2 * pair + 2, :], in_=result[:])
+                if not whole_store:
+                    nc.sync.dma_start(
+                        out=out_view[:, :, 2 * pair : 2 * pair + 2, :],
+                        in_=result[:, :, 2 * pair : 2 * pair + 2, :],
+                    )
+            if whole_store:
+                nc.sync.dma_start(out=out_view, in_=result[:])

@@ -90,38 +90,36 @@ def tile_refattention_pa_kernel(
         nc.scalar.dma_start(out=sin_sb[:], in_=sin_dram)
         nc.scalar.activation(out=warm[:], in_=one[:], func=ACT.Abs_reciprocal_sqrt)
 
-        for j in range(TOKEN_TILES):
-            nc.sync.dma_start(out=x_sb[:, j, :], in_=x_dram[:, j, :])
+        nc.sync.dma_start(out=x_sb[:, 0, :], in_=x_dram[:, 0, :])
+        nc.sync.dma_start(out=x_sb[:, 1, :], in_=x_dram[:, 1, :])
+        nc.sync.dma_start(out=x_sb[:, 2:4, :], in_=x_dram[:, 2:4, :])
 
-        def load_scales(scales, first_feature, features):
+        def load_scales(scales, first_feature, first_column, columns):
             for quadrant in range(4):
                 nc.sync.dma_start(
                     out=w_planes[
-                        32 * quadrant : 32 * quadrant + 16, first_feature : first_feature + features
+                        32 * quadrant : 32 * quadrant + 16, first_feature : first_feature + columns
                     ].bitcast(I32),
-                    in_=scales[:, 4 * quadrant : 4 * quadrant + 4, :].bitcast(I32),
+                    in_=scales[
+                        :, 4 * quadrant : 4 * quadrant + 4, first_column : first_column + columns
+                    ].bitcast(I32),
                 )
 
-        def load_words(words, first_feature, first_column, columns, by_pass=False):
+        def load_words(words, first_feature, first_column, columns):
             by_partition = words.rearrange("g p n t -> p g (n t)")
-            if by_pass:
-                for g in range(PASSES):
-                    nc.sync.dma_start(
-                        out=w_words[:, g, first_feature : first_feature + columns].bitcast(I32),
-                        in_=by_partition[:, g, 4 * first_column : 4 * (first_column + columns)].bitcast(I32),
-                    )
-            else:
-                nc.sync.dma_start(
-                    out=w_words[:, :, first_feature : first_feature + columns].bitcast(I32),
-                    in_=by_partition[:, :, 4 * first_column : 4 * (first_column + columns)].bitcast(I32),
-                )
+            nc.sync.dma_start(
+                out=w_words[:, :, first_feature : first_feature + columns].bitcast(I32),
+                in_=by_partition[:, :, 4 * first_column : 4 * (first_column + columns)].bitcast(I32),
+            )
 
-        load_scales(Wq_scales, 0, Q_FEATURES)
-        load_words(Wq_words, 0, 0, BANK, by_pass=True)
+        load_scales(Wq_scales, 0, 0, BANK)
+        load_words(Wq_words, 0, 0, BANK // 2)
+        load_words(Wq_words, BANK // 2, BANK // 2, BANK // 2)
+        load_scales(Wq_scales, BANK, BANK, Q_FEATURES - BANK)
         load_words(Wq_words, BANK, BANK, BANK)
         load_words(Wq_words, 2 * BANK, 2 * BANK, 2 * BANK)
-        load_scales(Wk_scales, Q_FEATURES, KV_FEATURES)
-        load_scales(Wv_scales, Q_FEATURES + KV_FEATURES, KV_FEATURES)
+        load_scales(Wk_scales, Q_FEATURES, 0, KV_FEATURES)
+        load_scales(Wv_scales, Q_FEATURES + KV_FEATURES, 0, KV_FEATURES)
         load_words(Wk_words, Q_FEATURES, 0, KV_FEATURES)
         load_words(Wv_words, Q_FEATURES + KV_FEATURES, 0, KV_FEATURES)
 
@@ -191,50 +189,53 @@ def tile_refattention_pa_kernel(
             for pair in range(TOKEN_TILES // 2):
                 if rotary:
                     products = work.tile([P, HEADS_PER_BANK, 4, D], F32, name="products")
-                for jj in range(2):
-                    j = 2 * pair + jj
-                    acc = psum.tile([P, HEADS_PER_BANK, D], F32, tag="bank", name="acc")
-                    for g in range(PASSES):
-                        nc.tensor.matmul_mx(
-                            out=acc[:].rearrange("p h d -> p (h d)"),
-                            lhsT=x_codes[:, j, g, :].bitcast(FP8X4),
-                            lhsT_scale=x_planes[:, j, g, :],
-                            rhs=w_words[:, g, BANK * group : BANK * (group + 1)].bitcast(FP8X4),
-                            rhs_scale=w_planes[4 * g : P, BANK * group : BANK * (group + 1)],
-                            start=(g == 0),
-                            stop=(g == PASSES - 1),
-                        )
-                    squares = junk.tile([P, HEADS_PER_BANK, D], F32, name="squares")
-                    sum_sq = small.tile([P, HEADS_PER_BANK], F32, name="sum_sq")
-                    for h in range(HEADS_PER_BANK):
-                        nc.scalar.activation(
-                            out=squares[:, h, :],
-                            in_=acc[:, h, :],
-                            func=ACT.Square,
-                            accum_out=sum_sq[:, h : h + 1],
-                        )
-                    rstd = small.tile([P, HEADS_PER_BANK], F32, name="rstd")
-                    nc.scalar.activation(
-                        out=rstd[:], in_=sum_sq[:], func=ACT.Abs_reciprocal_sqrt, scale=1.0 / D, bias=EPS
-                    )
-                    if rotary:
-                        which = 0 if group < Q_GROUPS else 1
-                        for h in range(HEADS_PER_BANK):
-                            nc.vector.scalar_tensor_tensor(
-                                out=products[:, h, jj : 4 - jj : 3 - 2 * jj, :],
-                                in0=acc[:, h, :].unsqueeze(1).to_broadcast([P, 2, D]),
-                                scalar=rstd[:, h : h + 1],
-                                in1=rope[:, j, which, :, :],
-                                op0=ALU.mult,
-                                op1=ALU.mult,
+                heads = HEADS_PER_BANK // 2 if group == 0 else HEADS_PER_BANK
+                for first_head in range(0, HEADS_PER_BANK, heads):
+                    first_feature = BANK * group + D * first_head
+                    for jj in range(2):
+                        j = 2 * pair + jj
+                        acc = psum.tile([P, heads, D], F32, tag="bank", name="acc")
+                        for g in range(PASSES):
+                            nc.tensor.matmul_mx(
+                                out=acc[:].rearrange("p h d -> p (h d)"),
+                                lhsT=x_codes[:, j, g, :].bitcast(FP8X4),
+                                lhsT_scale=x_planes[:, j, g, :],
+                                rhs=w_words[:, g, first_feature : first_feature + D * heads].bitcast(FP8X4),
+                                rhs_scale=w_planes[4 * g : P, first_feature : first_feature + D * heads],
+                                start=(g == 0),
+                                stop=(g == PASSES - 1),
                             )
-                    else:
-                        nc.vector.tensor_tensor(
-                            out=result[:, :, j, :],
-                            in0=acc[:],
-                            in1=rstd[:].unsqueeze(2).to_broadcast([P, HEADS_PER_BANK, D]),
-                            op=ALU.mult,
+                        squares = junk.tile([P, heads, D], F32, name="squares", tag="squares")
+                        sum_sq = small.tile([P, heads], F32, name="sum_sq", tag="sum_sq")
+                        for h in range(heads):
+                            nc.scalar.activation(
+                                out=squares[:, h, :],
+                                in_=acc[:, h, :],
+                                func=ACT.Square,
+                                accum_out=sum_sq[:, h : h + 1],
+                            )
+                        rstd = small.tile([P, heads], F32, name="rstd", tag="rstd")
+                        nc.scalar.activation(
+                            out=rstd[:], in_=sum_sq[:], func=ACT.Abs_reciprocal_sqrt, scale=1.0 / D, bias=EPS
                         )
+                        if rotary:
+                            which = 0 if group < Q_GROUPS else 1
+                            for h in range(heads):
+                                nc.vector.scalar_tensor_tensor(
+                                    out=products[:, first_head + h, jj : 4 - jj : 3 - 2 * jj, :],
+                                    in0=acc[:, h, :].unsqueeze(1).to_broadcast([P, 2, D]),
+                                    scalar=rstd[:, h : h + 1],
+                                    in1=rope[:, j, which, :, :],
+                                    op0=ALU.mult,
+                                    op1=ALU.mult,
+                                )
+                        else:
+                            nc.vector.tensor_tensor(
+                                out=result[:, :, j, :],
+                                in0=acc[:],
+                                in1=rstd[:].unsqueeze(2).to_broadcast([P, HEADS_PER_BANK, D]),
+                                op=ALU.mult,
+                            )
                 if rotary:
                     halves = products[:].rearrange("p h q (f i) -> p h (q f) i", f=2)
                     nc.gpsimd.tensor_tensor(

@@ -74,23 +74,24 @@ def tile_refattention_pa_kernel(
         x_codes = keep.tile([P, TOKEN_TILES, PASSES, P], U32, name="x_codes", align_bytes=64)
         x_planes = keep.tile([P, TOKEN_TILES, PASSES, P], U8, name="x_planes", align_bytes=64)
         rope = keep.tile([P, TOKEN_TILES, 2, 2, D], F32, name="rope")
+        minus_gain = keep.tile([P, 2, HALF], F32, name="minus_gain")
         ident = keep.tile([P, P], F32, name="ident")
         one = keep.tile([P, 1], F32, name="one")
         warm = keep.tile([P, 1], F32, name="warm")
 
-        nc.vector.memset(w_planes[:].bitcast(I32), 0)
-        nc.vector.memset(one[:], 1.0)
         nc.vector.memset(gain_rows[:], 0.0)
         nc.vector.memset(ones[:], 1.0)
+        nc.vector.memset(w_planes[:].bitcast(I32), 0)
+        nc.vector.memset(one[:], 1.0)
         make_identity(nc, ident[:])
 
-        nc.scalar.dma_start(out=gain_rows[0:1, 0, :], in_=q_norm_w.rearrange("(o d) -> o d", o=1))
-        nc.scalar.dma_start(out=gain_rows[0:1, 1, :], in_=k_norm_w.rearrange("(o d) -> o d", o=1))
         nc.scalar.dma_start(out=cos_sb[:], in_=cos_dram)
         nc.scalar.dma_start(out=sin_sb[:], in_=sin_dram)
         nc.scalar.activation(out=warm[:], in_=one[:], func=ACT.Abs_reciprocal_sqrt)
 
         nc.sync.dma_start(out=x_sb[:, 0, :], in_=x_dram[:, 0, :])
+        nc.sync.dma_start(out=gain_rows[0:1, 0, :], in_=q_norm_w.rearrange("(o d) -> o d", o=1))
+        nc.sync.dma_start(out=gain_rows[0:1, 1, :], in_=k_norm_w.rearrange("(o d) -> o d", o=1))
         nc.sync.dma_start(out=x_sb[:, 1, :], in_=x_dram[:, 1, :])
         nc.sync.dma_start(out=x_sb[:, 2:4, :], in_=x_dram[:, 2:4, :])
 
@@ -123,6 +124,34 @@ def tile_refattention_pa_kernel(
         load_words(Wk_words, Q_FEATURES, 0, KV_FEATURES)
         load_words(Wv_words, Q_FEATURES + KV_FEATURES, 0, KV_FEATURES)
 
+        gain = psum.tile([P, 2, D], F32, tag="bank", name="gain")
+        nc.tensor.matmul(
+            out=gain[:].rearrange("p w d -> p (w d)"),
+            lhsT=ones[:],
+            rhs=gain_rows[:].rearrange("p w d -> p (w d)"),
+            start=True,
+            stop=True,
+        )
+        nc.vector.tensor_tensor(
+            out=rope[:, :, :, 0, :],
+            in0=cos_sb[:].unsqueeze(2).to_broadcast([P, TOKEN_TILES, 2, D]),
+            in1=gain[:].unsqueeze(1).to_broadcast([P, TOKEN_TILES, 2, D]),
+            op=ALU.mult,
+        )
+        nc.vector.tensor_tensor(
+            out=rope[:, :, :, 1, 0:HALF],
+            in0=sin_sb[:, :, HALF:D].unsqueeze(2).to_broadcast([P, TOKEN_TILES, 2, HALF]),
+            in1=gain[:, :, 0:HALF].unsqueeze(1).to_broadcast([P, TOKEN_TILES, 2, HALF]),
+            op=ALU.mult,
+        )
+        nc.vector.tensor_scalar_mul(out=minus_gain[:], in0=gain[:, :, HALF:D], scalar1=-1.0)
+        nc.vector.tensor_tensor(
+            out=rope[:, :, :, 1, HALF:D],
+            in0=sin_sb[:, :, 0:HALF].unsqueeze(2).to_broadcast([P, TOKEN_TILES, 2, HALF]),
+            in1=minus_gain[:].unsqueeze(1).to_broadcast([P, TOKEN_TILES, 2, HALF]),
+            op=ALU.mult,
+        )
+
         for j in range(TOKEN_TILES):
             x_words = x_sb[:, j, :].bitcast(F32)
             for pair in range(PASSES // 2):
@@ -147,36 +176,6 @@ def tile_refattention_pa_kernel(
                     scales=x_planes[:, j, 2 * pair : 2 * pair + 2, :].rearrange("p g r -> p (g r)"),
                     in_=grouped[:].rearrange("p g r t -> p (g r t)"),
                 )
-
-        gain = psum.tile([P, 2, D], F32, tag="bank", name="gain")
-        nc.tensor.matmul(
-            out=gain[:].rearrange("p w d -> p (w d)"),
-            lhsT=ones[:],
-            rhs=gain_rows[:].rearrange("p w d -> p (w d)"),
-            start=True,
-            stop=True,
-        )
-        for j in range(TOKEN_TILES):
-            nc.vector.tensor_tensor(
-                out=rope[:, j, :, 0, :],
-                in0=cos_sb[:, j, :].unsqueeze(1).to_broadcast([P, 2, D]),
-                in1=gain[:],
-                op=ALU.mult,
-            )
-            nc.vector.tensor_tensor(
-                out=rope[:, j, :, 1, 0:HALF],
-                in0=sin_sb[:, j, HALF:D].unsqueeze(1).to_broadcast([P, 2, HALF]),
-                in1=gain[:, :, 0:HALF],
-                op=ALU.mult,
-            )
-            nc.vector.scalar_tensor_tensor(
-                out=rope[:, j, :, 1, HALF:D],
-                in0=sin_sb[:, j, 0:HALF].unsqueeze(1).to_broadcast([P, 2, HALF]),
-                scalar=-1.0,
-                in1=gain[:, :, HALF:D],
-                op0=ALU.mult,
-                op1=ALU.mult,
-            )
 
         out_views = [
             out_0[:, HEADS_PER_BANK * group : HEADS_PER_BANK * (group + 1)] for group in range(Q_GROUPS)

@@ -85,15 +85,16 @@ def tile_refattention_pa_kernel(
         nc.vector.memset(one[:], 1.0)
         make_identity(nc, ident[:])
 
-        nc.scalar.dma_start(out=cos_sb[:], in_=cos_dram)
-        nc.scalar.dma_start(out=sin_sb[:], in_=sin_dram)
         nc.scalar.activation(out=warm[:], in_=one[:], func=ACT.Abs_reciprocal_sqrt)
 
-        nc.sync.dma_start(out=x_sb[:, 0, :], in_=x_dram[:, 0, :])
+        nc.sync.dma_start(out=x_sb[:, 0, 0 : HID // 2], in_=x_dram[:, 0, 0 : HID // 2])
+        nc.sync.dma_start(out=x_sb[:, 0, HID // 2 : HID], in_=x_dram[:, 0, HID // 2 : HID])
+        nc.sync.dma_start(out=cos_sb[:], in_=cos_dram)
+        nc.sync.dma_start(out=sin_sb[:], in_=sin_dram)
         nc.sync.dma_start(out=gain_rows[0:1, 0, :], in_=q_norm_w.rearrange("(o d) -> o d", o=1))
         nc.sync.dma_start(out=gain_rows[0:1, 1, :], in_=k_norm_w.rearrange("(o d) -> o d", o=1))
-        nc.sync.dma_start(out=x_sb[:, 1, :], in_=x_dram[:, 1, :])
-        nc.sync.dma_start(out=x_sb[:, 2:4, :], in_=x_dram[:, 2:4, :])
+        for j in range(1, TOKEN_TILES):
+            nc.sync.dma_start(out=x_sb[:, j, :], in_=x_dram[:, j, :])
 
         def load_scales(scales, first_feature, first_column, columns):
             for quadrant in range(4):
@@ -124,35 +125,38 @@ def tile_refattention_pa_kernel(
         load_words(Wk_words, Q_FEATURES, 0, KV_FEATURES)
         load_words(Wv_words, Q_FEATURES + KV_FEATURES, 0, KV_FEATURES)
 
-        gain = psum.tile([P, 2, D], F32, tag="bank", name="gain")
-        nc.tensor.matmul(
-            out=gain[:].rearrange("p w d -> p (w d)"),
-            lhsT=ones[:],
-            rhs=gain_rows[:].rearrange("p w d -> p (w d)"),
-            start=True,
-            stop=True,
-        )
-        nc.vector.tensor_tensor(
-            out=rope[:, :, :, 0, :],
-            in0=cos_sb[:].unsqueeze(2).to_broadcast([P, TOKEN_TILES, 2, D]),
-            in1=gain[:].unsqueeze(1).to_broadcast([P, TOKEN_TILES, 2, D]),
-            op=ALU.mult,
-        )
-        nc.vector.tensor_tensor(
-            out=rope[:, :, :, 1, 0:HALF],
-            in0=sin_sb[:, :, HALF:D].unsqueeze(2).to_broadcast([P, TOKEN_TILES, 2, HALF]),
-            in1=gain[:, :, 0:HALF].unsqueeze(1).to_broadcast([P, TOKEN_TILES, 2, HALF]),
-            op=ALU.mult,
-        )
-        nc.vector.tensor_scalar_mul(out=minus_gain[:], in0=gain[:, :, HALF:D], scalar1=-1.0)
-        nc.vector.tensor_tensor(
-            out=rope[:, :, :, 1, HALF:D],
-            in0=sin_sb[:, :, 0:HALF].unsqueeze(2).to_broadcast([P, TOKEN_TILES, 2, HALF]),
-            in1=minus_gain[:].unsqueeze(1).to_broadcast([P, TOKEN_TILES, 2, HALF]),
-            op=ALU.mult,
-        )
+        def make_tables():
+            gain = psum.tile([P, 2, D], F32, tag="bank", name="gain")
+            nc.tensor.matmul(
+                out=gain[:].rearrange("p w d -> p (w d)"),
+                lhsT=ones[:],
+                rhs=gain_rows[:].rearrange("p w d -> p (w d)"),
+                start=True,
+                stop=True,
+            )
+            nc.vector.tensor_tensor(
+                out=rope[:, :, :, 0, :],
+                in0=cos_sb[:].unsqueeze(2).to_broadcast([P, TOKEN_TILES, 2, D]),
+                in1=gain[:].unsqueeze(1).to_broadcast([P, TOKEN_TILES, 2, D]),
+                op=ALU.mult,
+            )
+            nc.vector.tensor_tensor(
+                out=rope[:, :, :, 1, 0:HALF],
+                in0=sin_sb[:, :, HALF:D].unsqueeze(2).to_broadcast([P, TOKEN_TILES, 2, HALF]),
+                in1=gain[:, :, 0:HALF].unsqueeze(1).to_broadcast([P, TOKEN_TILES, 2, HALF]),
+                op=ALU.mult,
+            )
+            nc.vector.tensor_scalar_mul(out=minus_gain[:], in0=gain[:, :, HALF:D], scalar1=-1.0)
+            nc.vector.tensor_tensor(
+                out=rope[:, :, :, 1, HALF:D],
+                in0=sin_sb[:, :, 0:HALF].unsqueeze(2).to_broadcast([P, TOKEN_TILES, 2, HALF]),
+                in1=minus_gain[:].unsqueeze(1).to_broadcast([P, TOKEN_TILES, 2, HALF]),
+                op=ALU.mult,
+            )
 
         for j in range(TOKEN_TILES):
+            if j == 1:
+                make_tables()
             x_words = x_sb[:, j, :].bitcast(F32)
             for pair in range(PASSES // 2):
                 turned = psum.tile([P, 2, 2, P], F32, tag="bank", name="turned")

@@ -184,62 +184,106 @@ def tile_refattention_pa_kernel(
         out_views = [
             out_0[:, HEADS_PER_BANK * group : HEADS_PER_BANK * (group + 1)] for group in range(Q_GROUPS)
         ] + [out_1, out_2]
+        half_heads = HEADS_PER_BANK // 2
         for group in range(GROUPS):
             out_view = out_views[group].rearrange("b h (p j) d -> p (b h) j d", j=TOKEN_TILES)
             rotary = group < GROUPS - 1
             whole_store = group < Q_GROUPS
             result = outs.tile([P, HEADS_PER_BANK, TOKEN_TILES, D], F32, name="result")
             for pair in range(TOKEN_TILES // 2):
-                if rotary:
-                    products = work.tile([P, HEADS_PER_BANK, 4, D], F32, name="products")
-                heads = HEADS_PER_BANK // 2 if group == 0 else HEADS_PER_BANK
-                for first_head in range(0, HEADS_PER_BANK, heads):
+                last_rotary = group == GROUPS - 2 and pair == 1
+                last_of_all = group == GROUPS - 1 and pair == 1
+                if group == 0:
+                    units = [(first, half_heads, jj) for first in (0, half_heads) for jj in range(2)]
+                elif last_of_all:
+                    units = [(0, HEADS_PER_BANK, 0), (0, half_heads, 1), (half_heads, half_heads, 1)]
+                else:
+                    units = [(0, HEADS_PER_BANK, 0), (0, HEADS_PER_BANK, 1)]
+                if rotary and not last_rotary:
+                    products = work.tile([P, HEADS_PER_BANK, 4, D], F32, name="products", tag="products")
+                for first_head, heads, jj in units:
                     first_feature = BANK * group + D * first_head
-                    for jj in range(2):
-                        j = 2 * pair + jj
-                        acc = psum.tile([P, heads, D], F32, tag="bank", name="acc")
-                        for g in range(PASSES):
-                            nc.tensor.matmul_mx(
-                                out=acc[:].rearrange("p h d -> p (h d)"),
-                                lhsT=x_codes[:, j, g, :].bitcast(FP8X4),
-                                lhsT_scale=x_planes[:, j, g, :],
-                                rhs=w_words[:, g, first_feature : first_feature + D * heads].bitcast(FP8X4),
-                                rhs_scale=w_planes[4 * g : P, first_feature : first_feature + D * heads],
-                                start=(g == 0),
-                                stop=(g == PASSES - 1),
-                            )
-                        squares = junk.tile([P, heads, D], F32, name="squares", tag="squares")
-                        sum_sq = small.tile([P, heads], F32, name="sum_sq", tag="sum_sq")
-                        for h in range(heads):
-                            nc.scalar.activation(
-                                out=squares[:, h, :],
-                                in_=acc[:, h, :],
-                                func=ACT.Square,
-                                accum_out=sum_sq[:, h : h + 1],
-                            )
-                        rstd = small.tile([P, heads], F32, name="rstd", tag="rstd")
-                        nc.scalar.activation(
-                            out=rstd[:], in_=sum_sq[:], func=ACT.Abs_reciprocal_sqrt, scale=1.0 / D, bias=EPS
+                    j = 2 * pair + jj
+                    acc = psum.tile([P, heads, D], F32, tag="bank", name="acc")
+                    for g in range(PASSES):
+                        nc.tensor.matmul_mx(
+                            out=acc[:].rearrange("p h d -> p (h d)"),
+                            lhsT=x_codes[:, j, g, :].bitcast(FP8X4),
+                            lhsT_scale=x_planes[:, j, g, :],
+                            rhs=w_words[:, g, first_feature : first_feature + D * heads].bitcast(FP8X4),
+                            rhs_scale=w_planes[4 * g : P, first_feature : first_feature + D * heads],
+                            start=(g == 0),
+                            stop=(g == PASSES - 1),
                         )
-                        if rotary:
-                            which = 0 if group < Q_GROUPS else 1
-                            for h in range(heads):
-                                nc.vector.scalar_tensor_tensor(
-                                    out=products[:, first_head + h, jj : 4 - jj : 3 - 2 * jj, :],
-                                    in0=acc[:, h, :].unsqueeze(1).to_broadcast([P, 2, D]),
-                                    scalar=rstd[:, h : h + 1],
-                                    in1=rope[:, j, which, :, :],
-                                    op0=ALU.mult,
-                                    op1=ALU.mult,
-                                )
-                        else:
-                            nc.vector.tensor_tensor(
-                                out=result[:, :, j, :],
-                                in0=acc[:],
-                                in1=rstd[:].unsqueeze(2).to_broadcast([P, HEADS_PER_BANK, D]),
-                                op=ALU.mult,
+                    squares = junk.tile([P, heads, D], F32, name="squares", tag="squares")
+                    sum_sq = small.tile([P, heads], F32, name="sum_sq", tag="sum_sq")
+                    for h in range(heads):
+                        nc.scalar.activation(
+                            out=squares[:, h, :],
+                            in_=acc[:, h, :],
+                            func=ACT.Square,
+                            accum_out=sum_sq[:, h : h + 1],
+                        )
+                    rstd = small.tile([P, heads], F32, name="rstd", tag="rstd")
+                    nc.scalar.activation(
+                        out=rstd[:], in_=sum_sq[:], func=ACT.Abs_reciprocal_sqrt, scale=1.0 / D, bias=EPS
+                    )
+                    if last_rotary:
+                        single = work.tile([P, HEADS_PER_BANK, 2, D], F32, name="single", tag="products")
+                        for h in range(heads):
+                            nc.vector.scalar_tensor_tensor(
+                                out=single[:, h, :, :],
+                                in0=acc[:, h, :].unsqueeze(1).to_broadcast([P, 2, D]),
+                                scalar=rstd[:, h : h + 1],
+                                in1=rope[:, j, 1, :, :],
+                                op0=ALU.mult,
+                                op1=ALU.mult,
                             )
-                if rotary:
+                        quarters = single[:].rearrange("p h s (f i) -> p h (s f) i", f=2)
+                        if jj == 0:
+                            nc.gpsimd.tensor_tensor(
+                                out=result[:, :, j, :].rearrange("p h (f i) -> p h f i", f=2),
+                                in0=quarters[:, :, 0:2, :],
+                                in1=quarters[:, :, 3:1:-1, :],
+                                op=ALU.add,
+                            )
+                        else:
+                            nc.vector.tensor_reduce(
+                                out=result[:, :, j, 0:HALF],
+                                in_=quarters[:, :, 0:4:3, :].rearrange("p h s i -> p h i s"),
+                                axis=mybir.AxisListType.X,
+                                op=ALU.add,
+                            )
+                            nc.vector.tensor_reduce(
+                                out=result[:, :, j, HALF:D],
+                                in_=quarters[:, :, 1:3, :].rearrange("p h s i -> p h i s"),
+                                axis=mybir.AxisListType.X,
+                                op=ALU.add,
+                            )
+                    elif rotary:
+                        which = 0 if group < Q_GROUPS else 1
+                        for h in range(heads):
+                            nc.vector.scalar_tensor_tensor(
+                                out=products[:, first_head + h, jj : 4 - jj : 3 - 2 * jj, :],
+                                in0=acc[:, h, :].unsqueeze(1).to_broadcast([P, 2, D]),
+                                scalar=rstd[:, h : h + 1],
+                                in1=rope[:, j, which, :, :],
+                                op0=ALU.mult,
+                                op1=ALU.mult,
+                            )
+                    else:
+                        nc.vector.tensor_tensor(
+                            out=result[:, first_head : first_head + heads, j, :],
+                            in0=acc[:],
+                            in1=rstd[:].unsqueeze(2).to_broadcast([P, heads, D]),
+                            op=ALU.mult,
+                        )
+                        if last_of_all and jj == 1:
+                            nc.sync.dma_start(
+                                out=out_view[:, first_head : first_head + heads, 2 * pair : 2 * pair + 2, :],
+                                in_=result[:, first_head : first_head + heads, 2 * pair : 2 * pair + 2, :],
+                            )
+                if rotary and not last_rotary:
                     halves = products[:].rearrange("p h q (f i) -> p h (q f) i", f=2)
                     nc.gpsimd.tensor_tensor(
                         out=result[:, :, 2 * pair : 2 * pair + 2, :].rearrange("p h j (f i) -> p h (j f) i", f=2),
@@ -247,7 +291,7 @@ def tile_refattention_pa_kernel(
                         in1=halves[:, :, 7:3:-1, :],
                         op=ALU.add,
                     )
-                if not whole_store:
+                if not whole_store and not last_of_all:
                     nc.sync.dma_start(
                         out=out_view[:, :, 2 * pair : 2 * pair + 2, :],
                         in_=result[:, :, 2 * pair : 2 * pair + 2, :],

from contextlib import ExitStack

import concourse.mybir as mybir
from concourse.masks import make_identity

F32 = mybir.dt.float32
BF16 = mybir.dt.bfloat16
I32 = mybir.dt.int32
U32 = mybir.dt.uint32
U8 = mybir.dt.uint8
FP8X4 = mybir.dt.float8_e4m3fn_x4
ACT = mybir.ActivationFunctionType
ALU = mybir.AluOpType

P = 128
TOKENS = 512
HID = 2048
D = 128
HALF = D // 2
EPS = 1e-6
K_PASS = 4 * P
PASSES = HID // K_PASS
TOKEN_TILES = TOKENS // P
BANK = 512
HEADS_PER_BANK = BANK // D
Q_FEATURES = 2048
KV_FEATURES = 512
FEATURES = Q_FEATURES + 2 * KV_FEATURES
GROUPS = FEATURES // BANK
Q_GROUPS = Q_FEATURES // BANK
WORDS_PER_PASS = K_PASS // 2

FLOPS = 2 * TOKENS * HID * FEATURES


def tile_refattention_pa_kernel(
    tc,
    hidden_states,
    cos,
    sin,
    Wq_words,
    Wq_scales,
    Wk_words,
    Wk_scales,
    Wv_words,
    Wv_scales,
    q_norm_w,
    k_norm_w,
    out_0,
    out_1,
    out_2,
):
    nc = tc.nc
    with ExitStack() as ctx:
        keep = ctx.enter_context(tc.tile_pool(name="keep", bufs=1))
        stage = ctx.enter_context(tc.tile_pool(name="stage", bufs=4))
        small = ctx.enter_context(tc.tile_pool(name="small", bufs=6))
        junk = ctx.enter_context(tc.tile_pool(name="junk", bufs=4))
        work = ctx.enter_context(tc.tile_pool(name="work", bufs=5))
        outs = ctx.enter_context(tc.tile_pool(name="outs", bufs=4))
        psum = ctx.enter_context(tc.psum_pool(name="psum", bufs=8))

        x_dram = hidden_states.rearrange("b (p j) k -> p (b j) k", j=TOKEN_TILES)
        cos_dram = cos.rearrange("b (p j) d -> p (b j) d", j=TOKEN_TILES)
        sin_dram = sin.rearrange("b (p j) d -> p (b j) d", j=TOKEN_TILES)

        x_sb = keep.tile([P, TOKEN_TILES, HID], BF16, name="x_sb")
        cos_sb = keep.tile([P, TOKEN_TILES, D], BF16, name="cos_sb")
        sin_sb = keep.tile([P, TOKEN_TILES, D], BF16, name="sin_sb")
        gain_rows = keep.tile([P, 2, D], BF16, name="gain_rows")
        ones = keep.tile([P, P], BF16, name="ones")
        w_words = keep.tile([P, PASSES, FEATURES], U32, name="w_words", align_bytes=64)
        w_planes = keep.tile([P, FEATURES], U8, name="w_planes", align_bytes=64)
        x_codes = keep.tile([P, TOKEN_TILES, PASSES, P], U32, name="x_codes", align_bytes=64)
        x_planes = keep.tile([P, TOKEN_TILES, PASSES, P], U8, name="x_planes", align_bytes=64)
        rope = keep.tile([P, TOKEN_TILES, 2, 2, D], F32, name="rope")
        minus_gain = keep.tile([P, 2, HALF], F32, name="minus_gain")
        ident = keep.tile([P, P], F32, name="ident")
        one = keep.tile([P, 1], F32, name="one")
        warm = keep.tile([P, 1], F32, name="warm")

        nc.vector.memset(gain_rows[:], 0.0)
        nc.vector.memset(ones[:], 1.0)
        nc.vector.memset(w_planes[:].bitcast(I32), 0)
        nc.vector.memset(one[:], 1.0)
        make_identity(nc, ident[:])

        nc.scalar.activation(out=warm[:], in_=one[:], func=ACT.Abs_reciprocal_sqrt)

        nc.sync.dma_start(out=x_sb[:, 0, 0 : HID // 2], in_=x_dram[:, 0, 0 : HID // 2])
        nc.sync.dma_start(out=x_sb[:, 0, HID // 2 : HID], in_=x_dram[:, 0, HID // 2 : HID])
        nc.sync.dma_start(out=cos_sb[:], in_=cos_dram)
        nc.sync.dma_start(out=sin_sb[:], in_=sin_dram)
        nc.sync.dma_start(out=gain_rows[0:1, 0, :], in_=q_norm_w.rearrange("(o d) -> o d", o=1))
        nc.sync.dma_start(out=gain_rows[0:1, 1, :], in_=k_norm_w.rearrange("(o d) -> o d", o=1))
        for j in range(1, TOKEN_TILES):
            nc.sync.dma_start(out=x_sb[:, j, :], in_=x_dram[:, j, :])

        def load_scales(scales, first_feature, first_column, columns):
            for quadrant in range(4):
                nc.sync.dma_start(
                    out=w_planes[
                        32 * quadrant : 32 * quadrant + 16, first_feature : first_feature + columns
                    ].bitcast(I32),
                    in_=scales[
                        :, 4 * quadrant : 4 * quadrant + 4, first_column : first_column + columns
                    ].bitcast(I32),
                )

        def load_words(words, first_feature, first_column, columns):
            by_partition = words.rearrange("g p n t -> p g (n t)")
            nc.sync.dma_start(
                out=w_words[:, :, first_feature : first_feature + columns].bitcast(I32),
                in_=by_partition[:, :, 4 * first_column : 4 * (first_column + columns)].bitcast(I32),
            )

        load_scales(Wq_scales, 0, 0, BANK)
        load_words(Wq_words, 0, 0, BANK // 2)
        load_words(Wq_words, BANK // 2, BANK // 2, BANK // 2)
        load_scales(Wq_scales, BANK, BANK, Q_FEATURES - BANK)
        load_words(Wq_words, BANK, BANK, BANK)
        load_words(Wq_words, 2 * BANK, 2 * BANK, 2 * BANK)
        load_scales(Wk_scales, Q_FEATURES, 0, KV_FEATURES)
        load_scales(Wv_scales, Q_FEATURES + KV_FEATURES, 0, KV_FEATURES)
        load_words(Wk_words, Q_FEATURES, 0, KV_FEATURES)
        load_words(Wv_words, Q_FEATURES + KV_FEATURES, 0, KV_FEATURES)

        def make_tables():
            gain = psum.tile([P, 2, D], F32, tag="bank", name="gain")
            nc.tensor.matmul(
                out=gain[:].rearrange("p w d -> p (w d)"),
                lhsT=ones[:],
                rhs=gain_rows[:].rearrange("p w d -> p (w d)"),
                start=True,
                stop=True,
            )
            nc.vector.tensor_tensor(
                out=rope[:, :, :, 0, :],
                in0=cos_sb[:].unsqueeze(2).to_broadcast([P, TOKEN_TILES, 2, D]),
                in1=gain[:].unsqueeze(1).to_broadcast([P, TOKEN_TILES, 2, D]),
                op=ALU.mult,
            )
            nc.vector.tensor_tensor(
                out=rope[:, :, :, 1, 0:HALF],
                in0=sin_sb[:, :, HALF:D].unsqueeze(2).to_broadcast([P, TOKEN_TILES, 2, HALF]),
                in1=gain[:, :, 0:HALF].unsqueeze(1).to_broadcast([P, TOKEN_TILES, 2, HALF]),
                op=ALU.mult,
            )
            nc.vector.tensor_scalar_mul(out=minus_gain[:], in0=gain[:, :, HALF:D], scalar1=-1.0)
            nc.vector.tensor_tensor(
                out=rope[:, :, :, 1, HALF:D],
                in0=sin_sb[:, :, 0:HALF].unsqueeze(2).to_broadcast([P, TOKEN_TILES, 2, HALF]),
                in1=minus_gain[:].unsqueeze(1).to_broadcast([P, TOKEN_TILES, 2, HALF]),
                op=ALU.mult,
            )

        for j in range(TOKEN_TILES):
            if j == 1:
                make_tables()
            x_words = x_sb[:, j, :].bitcast(F32)
            for pair in range(PASSES // 2):
                turned = psum.tile([P, 2, 2, P], F32, tag="bank", name="turned")
                for gi in range(2):
                    g = 2 * pair + gi
                    for u in range(2):
                        nc.tensor.transpose(
                            turned[:, gi, u, :],
                            x_words[:, WORDS_PER_PASS * g + u : WORDS_PER_PASS * (g + 1) : 2],
                            ident[:],
                        )
                grouped = stage.tile([P, 2, P, 4], BF16, name="grouped", align_bytes=64)
                nc.scalar.copy(
                    out=grouped[:].bitcast(F32),
                    in_=turned[:].rearrange("p g u r -> p g r u"),
                )
                nc.vector.quantize_mx(
                    out=x_codes[:, j, 2 * pair : 2 * pair + 2, :]
                    .rearrange("p g r -> p (g r)")
                    .bitcast(FP8X4),
                    scales=x_planes[:, j, 2 * pair : 2 * pair + 2, :].rearrange("p g r -> p (g r)"),
                    in_=grouped[:].rearrange("p g r t -> p (g r t)"),
                )

        out_views = [
            out_0[:, HEADS_PER_BANK * group : HEADS_PER_BANK * (group + 1)] for group in range(Q_GROUPS)
        ] + [out_1, out_2]
        half_heads = HEADS_PER_BANK // 2
        for group in range(GROUPS):
            out_view = out_views[group].rearrange("b h (p j) d -> p (b h) j d", j=TOKEN_TILES)
            rotary = group < GROUPS - 1
            whole_store = group < Q_GROUPS
            result = outs.tile([P, HEADS_PER_BANK, TOKEN_TILES, D], F32, name="result")
            for pair in range(TOKEN_TILES // 2):
                last_rotary = group == GROUPS - 2 and pair == 1
                last_of_all = group == GROUPS - 1 and pair == 1
                if group == 0:
                    units = [(first, half_heads, jj) for first in (0, half_heads) for jj in range(2)]
                elif last_of_all:
                    units = [(0, HEADS_PER_BANK, 0), (0, half_heads, 1), (half_heads, half_heads, 1)]
                else:
                    units = [(0, HEADS_PER_BANK, 0), (0, HEADS_PER_BANK, 1)]
                if rotary and not last_rotary:
                    products = work.tile([P, HEADS_PER_BANK, 4, D], F32, name="products", tag="products")
                for first_head, heads, jj in units:
                    first_feature = BANK * group + D * first_head
                    j = 2 * pair + jj
                    acc = psum.tile([P, heads, D], F32, tag="bank", name="acc")
                    for g in range(PASSES):
                        nc.tensor.matmul_mx(
                            out=acc[:].rearrange("p h d -> p (h d)"),
                            lhsT=x_codes[:, j, g, :].bitcast(FP8X4),
                            lhsT_scale=x_planes[:, j, g, :],
                            rhs=w_words[:, g, first_feature : first_feature + D * heads].bitcast(FP8X4),
                            rhs_scale=w_planes[4 * g : P, first_feature : first_feature + D * heads],
                            start=(g == 0),
                            stop=(g == PASSES - 1),
                        )
                    squares = junk.tile([P, heads, D], F32, name="squares", tag="squares")
                    sum_sq = small.tile([P, heads], F32, name="sum_sq", tag="sum_sq")
                    for h in range(heads):
                        nc.scalar.activation(
                            out=squares[:, h, :],
                            in_=acc[:, h, :],
                            func=ACT.Square,
                            accum_out=sum_sq[:, h : h + 1],
                        )
                    rstd = small.tile([P, heads], F32, name="rstd", tag="rstd")
                    nc.scalar.activation(
                        out=rstd[:], in_=sum_sq[:], func=ACT.Abs_reciprocal_sqrt, scale=1.0 / D, bias=EPS
                    )
                    if last_rotary:
                        single = work.tile([P, HEADS_PER_BANK, 2, D], F32, name="single", tag="products")
                        for h in range(heads):
                            nc.vector.scalar_tensor_tensor(
                                out=single[:, h, :, :],
                                in0=acc[:, h, :].unsqueeze(1).to_broadcast([P, 2, D]),
                                scalar=rstd[:, h : h + 1],
                                in1=rope[:, j, 1, :, :],
                                op0=ALU.mult,
                                op1=ALU.mult,
                            )
                        quarters = single[:].rearrange("p h s (f i) -> p h (s f) i", f=2)
                        if jj == 0:
                            nc.gpsimd.tensor_tensor(
                                out=result[:, :, j, :].rearrange("p h (f i) -> p h f i", f=2),
                                in0=quarters[:, :, 0:2, :],
                                in1=quarters[:, :, 3:1:-1, :],
                                op=ALU.add,
                            )
                        else:
                            nc.vector.tensor_reduce(
                                out=result[:, :, j, 0:HALF],
                                in_=quarters[:, :, 0:4:3, :].rearrange("p h s i -> p h i s"),
                                axis=mybir.AxisListType.X,
                                op=ALU.add,
                            )
                            nc.vector.tensor_reduce(
                                out=result[:, :, j, HALF:D],
                                in_=quarters[:, :, 1:3, :].rearrange("p h s i -> p h i s"),
                                axis=mybir.AxisListType.X,
                                op=ALU.add,
                            )
                    elif rotary:
                        which = 0 if group < Q_GROUPS else 1
                        for h in range(heads):
                            nc.vector.scalar_tensor_tensor(
                                out=products[:, first_head + h, jj : 4 - jj : 3 - 2 * jj, :],
                                in0=acc[:, h, :].unsqueeze(1).to_broadcast([P, 2, D]),
                                scalar=rstd[:, h : h + 1],
                                in1=rope[:, j, which, :, :],
                                op0=ALU.mult,
                                op1=ALU.mult,
                            )
                    else:
                        nc.vector.tensor_tensor(
                            out=result[:, first_head : first_head + heads, j, :],
                            in0=acc[:],
                            in1=rstd[:].unsqueeze(2).to_broadcast([P, heads, D]),
                            op=ALU.mult,
                        )
                        if last_of_all and jj == 1:
                            nc.sync.dma_start(
                                out=out_view[:, first_head : first_head + heads, 2 * pair : 2 * pair + 2, :],
                                in_=result[:, first_head : first_head + heads, 2 * pair : 2 * pair + 2, :],
                            )
                if rotary and not last_rotary:
                    halves = products[:].rearrange("p h q (f i) -> p h (q f) i", f=2)
                    nc.gpsimd.tensor_tensor(
                        out=result[:, :, 2 * pair : 2 * pair + 2, :].rearrange("p h j (f i) -> p h (j f) i", f=2),
                        in0=halves[:, :, 0:4, :],
                        in1=halves[:, :, 7:3:-1, :],
                        op=ALU.add,
                    )
                if not whole_store and not last_of_all:
                    nc.sync.dma_start(
                        out=out_view[:, :, 2 * pair : 2 * pair + 2, :],
                        in_=result[:, :, 2 * pair : 2 * pair + 2, :],
                    )
            if whole_store:
                nc.sync.dma_start(out=out_view, in_=result[:])
